import numpy as np
import ml_dtypes

BF16 = ml_dtypes.bfloat16


def bf(x):
    return np.asarray(x, np.float32).astype(BF16)


def f32(x):
    return np.asarray(x, np.float32)


def f64(x):
    return np.asarray(x).astype(np.float64)


def striped(idx):
    return np.tile(idx.reshape(-1, 16).T, (8, 1))


C, S, K, NB, BSZ, N, H, R = 256, 512, 8, 4, 2, 4096, 256, 16


def sigmoid(v):
    return 1.0 / (1.0 + np.exp(-v))


def setup_inputs():
    return {"x": f32(np.random.standard_normal((C, S))), "br_w": f32(np.random.standard_normal((C, N))), "w_logit": f32(np.random.standard_normal((1, N))), "grp_w": f32(np.random.standard_normal((C, S * NB))), "offs": striped(np.concatenate([np.random.permutation(S)[:H] for _ in range(R)]))}


def reference(x, br_w, w_logit, grp_w, offs):
    idx = offs[:16].T.reshape(-1)
    t = f64(x)[:, idx] * f64(br_w) * sigmoid(f64(w_logit))
    branch = np.tanh(t.reshape(C, S * NB, BSZ).sum(axis=-1))
    return np.tanh((branch * f64(grp_w)).reshape(C, S, NB).sum(axis=-1))

@@ -1,0 +1,82 @@
+import concourse.mybir as mybir
+
+F32 = mybir.dt.float32
+U16 = mybir.dt.uint16
+MULT = mybir.AluOpType.mult
+ADD = mybir.AluOpType.add
+SIGMOID = mybir.ActivationFunctionType.Sigmoid
+TANH = mybir.ActivationFunctionType.Tanh
+
+P = 128
+C = 256
+S = 512
+N = 4096
+PER_BRANCH = 2
+PER_GROUP = 4
+BLOCKS = C // P
+PIECE = S
+PIECES = N // PIECE
+BRANCHES = PIECE // PER_BRANCH
+NEURONS = BRANCHES // PER_GROUP
+
+
+def tile_memorygraph_kernel(tc, x, br_w, w_logit, grp_w, offs, out):
+    nc = tc.nc
+    with (
+        tc.tile_pool(name="held", bufs=1) as held,
+        tc.tile_pool(name="work", bufs=3) as work,
+    ):
+        offsets = held.tile([P, N // 16], U16, name="offsets")
+        nc.sync.dma_start(offsets[:], offs)
+
+        windows = [held.tile([P, S], F32, name=f"window{b}") for b in range(BLOCKS)]
+        branch_w = [held.tile([P, N], F32, name=f"branch_w{b}") for b in range(BLOCKS)]
+        group_w = [held.tile([P, N // PER_BRANCH], F32, name=f"group_w{b}") for b in range(BLOCKS)]
+        result = [held.tile([P, S], F32, name=f"result{b}") for b in range(BLOCKS)]
+        logits = held.tile([P, N], F32, name="logits")
+        gate = held.tile([P, N], F32, name="gate")
+
+        for b in range(BLOCKS):
+            nc.sync.dma_start(windows[b][:], x[b * P : (b + 1) * P, :])
+
+        logit_rows = w_logit.rearrange("o n -> (o n)").partition_broadcast(P)
+        for k in range(PIECES):
+            piece = slice(k * PIECE, (k + 1) * PIECE)
+            nc.scalar.dma_start(logits[:, piece], logit_rows[:, piece])
+            for b in range(BLOCKS):
+                nc.sync.dma_start(branch_w[b][:, piece], br_w[b * P : (b + 1) * P, piece])
+        for b in range(BLOCKS):
+            nc.scalar.dma_start(group_w[b][:], grp_w[b * P : (b + 1) * P, :])
+
+        for k in range(PIECES):
+            piece = slice(k * PIECE, (k + 1) * PIECE)
+            nc.scalar.activation(gate[:, piece], logits[:, piece], SIGMOID)
+            for b in range(BLOCKS):
+                weights = work.tile([P, PIECE], F32, name="weights")
+                nc.vector.tensor_tensor(weights[:], branch_w[b][:, piece], gate[:, piece], MULT)
+
+                picked = windows[b][:].indirect(offsets[:, k * (PIECE // 16) : (k + 1) * (PIECE // 16)])
+                weighted = work.tile([P, PIECE], F32, name="weighted")
+                nc.vector.tensor_tensor(weighted[:], picked, weights[:], MULT)
+
+                pairs = weighted[:].rearrange("p (q i) -> p q i", i=PER_BRANCH)
+                branch_sum = work.tile([P, BRANCHES], F32, name="branch_sum")
+                nc.vector.tensor_tensor(branch_sum[:], pairs[:, :, 0], pairs[:, :, 1], ADD)
+                branch = work.tile([P, BRANCHES], F32, name="branch")
+                nc.scalar.activation(branch[:], branch_sum[:], TANH)
+
+                grouped = work.tile([P, BRANCHES], F32, name="grouped")
+                nc.vector.tensor_tensor(
+                    grouped[:], branch[:], group_w[b][:, k * BRANCHES : (k + 1) * BRANCHES], MULT
+                )
+                group_sum = work.tile([P, NEURONS], F32, name="group_sum")
+                nc.vector.tensor_reduce(
+                    group_sum[:],
+                    grouped[:].rearrange("p (n r) -> p n r", r=PER_GROUP),
+                    mybir.AxisListType.X,
+                    ADD,
+                )
+                nc.scalar.activation(result[b][:, k * NEURONS : (k + 1) * NEURONS], group_sum[:], TANH)
+
+        for b in range(BLOCKS):
+            nc.sync.dma_start(out[b * P : (b + 1) * P, :], result[b][:])

@@ -1,4 +1,5 @@
 import concourse.mybir as mybir
+from concourse.masks import make_identity
 
 F32 = mybir.dt.float32
 U16 = mybir.dt.uint16
@@ -25,58 +26,58 @@ def tile_memorygraph_kernel(tc, x, br_w, w_logit, grp_w, offs, out):
     with (
         tc.tile_pool(name="held", bufs=1) as held,
         tc.tile_pool(name="work", bufs=3) as work,
+        tc.psum_pool(name="sums", bufs=3) as sums,
     ):
         offsets = held.tile([P, N // 16], U16, name="offsets")
         nc.sync.dma_start(offsets[:], offs)
 
-        windows = [held.tile([P, S], F32, name=f"window{b}") for b in range(BLOCKS)]
-        branch_w = [held.tile([P, N], F32, name=f"branch_w{b}") for b in range(BLOCKS)]
-        group_w = [held.tile([P, N // PER_BRANCH], F32, name=f"group_w{b}") for b in range(BLOCKS)]
-        result = [held.tile([P, S], F32, name=f"result{b}") for b in range(BLOCKS)]
-        logits = held.tile([P, N], F32, name="logits")
-        gate = held.tile([P, N], F32, name="gate")
-
-        for b in range(BLOCKS):
-            nc.sync.dma_start(windows[b][:], x[b * P : (b + 1) * P, :])
-
         logit_rows = w_logit.rearrange("o n -> (o n)").partition_broadcast(P)
-        for k in range(PIECES):
-            piece = slice(k * PIECE, (k + 1) * PIECE)
-            nc.scalar.dma_start(logits[:, piece], logit_rows[:, piece])
-            for b in range(BLOCKS):
-                nc.sync.dma_start(branch_w[b][:, piece], br_w[b * P : (b + 1) * P, piece])
+        windows, branch_w, group_w, logits = [], [], [], []
         for b in range(BLOCKS):
-            nc.scalar.dma_start(group_w[b][:], grp_w[b * P : (b + 1) * P, :])
+            rows = slice(b * P, (b + 1) * P)
+            windows.append(held.tile([P, S], F32, name=f"window{b}"))
+            nc.sync.dma_start(windows[b][:], x[rows, :])
+            branch_w.append([held.tile([P, PIECE], F32, name=f"branch_w{b}_{k}") for k in range(PIECES)])
+            group_w.append([held.tile([P, BRANCHES], F32, name=f"group_w{b}_{k}") for k in range(PIECES)])
+            for k in range(PIECES):
+                if b == 0:
+                    logits.append(held.tile([P, PIECE], F32, name=f"logits{k}"))
+                    nc.sync.dma_start(logits[k][:], logit_rows[:, k * PIECE : (k + 1) * PIECE])
+                nc.sync.dma_start(branch_w[b][k][:], br_w[rows, k * PIECE : (k + 1) * PIECE])
+                nc.sync.dma_start(group_w[b][k][:], grp_w[rows, k * BRANCHES : (k + 1) * BRANCHES])
 
-        for k in range(PIECES):
-            piece = slice(k * PIECE, (k + 1) * PIECE)
-            nc.scalar.activation(gate[:, piece], logits[:, piece], SIGMOID)
-            for b in range(BLOCKS):
+        identity = held.tile([P, P], F32, name="identity")
+        make_identity(nc, identity[:])
+
+        gate = [held.tile([P, PIECE], F32, name=f"gate{k}") for k in range(PIECES)]
+        for b in range(BLOCKS):
+            result = held.tile([P, S], F32, name=f"result{b}")
+            for k in range(PIECES):
+                if b == 0:
+                    nc.scalar.activation(gate[k][:], logits[k][:], SIGMOID)
                 weights = work.tile([P, PIECE], F32, name="weights")
-                nc.vector.tensor_tensor(weights[:], branch_w[b][:, piece], gate[:, piece], MULT)
+                nc.vector.tensor_tensor(weights[:], branch_w[b][k][:], gate[k][:], MULT)
 
                 picked = windows[b][:].indirect(offsets[:, k * (PIECE // 16) : (k + 1) * (PIECE // 16)])
                 weighted = work.tile([P, PIECE], F32, name="weighted")
                 nc.vector.tensor_tensor(weighted[:], picked, weights[:], MULT)
 
                 pairs = weighted[:].rearrange("p (q i) -> p q i", i=PER_BRANCH)
-                branch_sum = work.tile([P, BRANCHES], F32, name="branch_sum")
-                nc.vector.tensor_tensor(branch_sum[:], pairs[:, :, 0], pairs[:, :, 1], ADD)
+                branch_sum = sums.tile([P, BRANCHES], F32, name="branch_sum")
+                for i in range(PER_BRANCH):
+                    nc.tensor.matmul(
+                        branch_sum[:], identity[:], pairs[:, :, i], start=(i == 0), stop=(i == PER_BRANCH - 1)
+                    )
                 branch = work.tile([P, BRANCHES], F32, name="branch")
                 nc.scalar.activation(branch[:], branch_sum[:], TANH)
 
                 grouped = work.tile([P, BRANCHES], F32, name="grouped")
-                nc.vector.tensor_tensor(
-                    grouped[:], branch[:], group_w[b][:, k * BRANCHES : (k + 1) * BRANCHES], MULT
-                )
-                group_sum = work.tile([P, NEURONS], F32, name="group_sum")
-                nc.vector.tensor_reduce(
-                    group_sum[:],
-                    grouped[:].rearrange("p (n r) -> p n r", r=PER_GROUP),
-                    mybir.AxisListType.X,
-                    ADD,
-                )
-                nc.scalar.activation(result[b][:, k * NEURONS : (k + 1) * NEURONS], group_sum[:], TANH)
-
-        for b in range(BLOCKS):
-            nc.sync.dma_start(out[b * P : (b + 1) * P, :], result[b][:])
+                nc.vector.tensor_tensor(grouped[:], branch[:], group_w[b][k][:], MULT)
+                quads = grouped[:].rearrange("p (n r) -> p n r", r=PER_GROUP)
+                group_sum = sums.tile([P, NEURONS], F32, name="group_sum")
+                for r in range(PER_GROUP):
+                    nc.tensor.matmul(
+                        group_sum[:], identity[:], quads[:, :, r], start=(r == 0), stop=(r == PER_GROUP - 1)
+                    )
+                nc.scalar.activation(result[:, k * NEURONS : (k + 1) * NEURONS], group_sum[:], TANH)
+            nc.sync.dma_start(out[b * P : (b + 1) * P, :], result[:])

@@ -19,13 +19,15 @@ PIECE = S
 PIECES = N // PIECE
 BRANCHES = PIECE // PER_BRANCH
 NEURONS = BRANCHES // PER_GROUP
+STEPS = BLOCKS * PIECES
+BEHIND = 2
 
 
 def tile_memorygraph_kernel(tc, x, br_w, w_logit, grp_w, offs, out):
     nc = tc.nc
     with (
         tc.tile_pool(name="held", bufs=1) as held,
-        tc.tile_pool(name="work", bufs=3) as work,
+        tc.tile_pool(name="work", bufs=4) as work,
         tc.psum_pool(name="sums", bufs=3) as sums,
     ):
         offsets = held.tile([P, N // 16], U16, name="offsets")
@@ -50,34 +52,54 @@ def tile_memorygraph_kernel(tc, x, br_w, w_logit, grp_w, offs, out):
         make_identity(nc, identity[:])
 
         gate = [held.tile([P, PIECE], F32, name=f"gate{k}") for k in range(PIECES)]
-        for b in range(BLOCKS):
-            result = held.tile([P, S], F32, name=f"result{b}")
-            for k in range(PIECES):
-                if b == 0:
-                    nc.scalar.activation(gate[k][:], logits[k][:], SIGMOID)
-                weights = work.tile([P, PIECE], F32, name="weights")
-                nc.vector.tensor_tensor(weights[:], branch_w[b][k][:], gate[k][:], MULT)
+        result = [held.tile([P, S], F32, name=f"result{b}") for b in range(BLOCKS)]
+        weights, branch = {}, {}
 
-                picked = windows[b][:].indirect(offsets[:, k * (PIECE // 16) : (k + 1) * (PIECE // 16)])
-                weighted = work.tile([P, PIECE], F32, name="weighted")
-                nc.vector.tensor_tensor(weighted[:], picked, weights[:], MULT)
+        def make_gate(k):
+            nc.scalar.activation(gate[k][:], logits[k][:], SIGMOID)
 
-                pairs = weighted[:].rearrange("p (q i) -> p q i", i=PER_BRANCH)
-                branch_sum = sums.tile([P, BRANCHES], F32, name="branch_sum")
-                for i in range(PER_BRANCH):
-                    nc.tensor.matmul(
-                        branch_sum[:], identity[:], pairs[:, :, i], start=(i == 0), stop=(i == PER_BRANCH - 1)
-                    )
-                branch = work.tile([P, BRANCHES], F32, name="branch")
-                nc.scalar.activation(branch[:], branch_sum[:], TANH)
+        def make_weights(s):
+            b, k = divmod(s, PIECES)
+            weights[s] = work.tile([P, PIECE], F32, name="weights")
+            nc.vector.tensor_tensor(weights[s][:], branch_w[b][k][:], gate[k][:], MULT)
 
-                grouped = work.tile([P, BRANCHES], F32, name="grouped")
-                nc.vector.tensor_tensor(grouped[:], branch[:], group_w[b][k][:], MULT)
-                quads = grouped[:].rearrange("p (n r) -> p n r", r=PER_GROUP)
-                group_sum = sums.tile([P, NEURONS], F32, name="group_sum")
-                for r in range(PER_GROUP):
-                    nc.tensor.matmul(
-                        group_sum[:], identity[:], quads[:, :, r], start=(r == 0), stop=(r == PER_GROUP - 1)
-                    )
-                nc.scalar.activation(result[:, k * NEURONS : (k + 1) * NEURONS], group_sum[:], TANH)
-            nc.sync.dma_start(out[b * P : (b + 1) * P, :], result[:])
+        def make_branches(s):
+            b, k = divmod(s, PIECES)
+            picked = windows[b][:].indirect(offsets[:, k * (PIECE // 16) : (k + 1) * (PIECE // 16)])
+            weighted = work.tile([P, PIECE], F32, name="weighted")
+            nc.vector.tensor_tensor(weighted[:], picked, weights[s][:], MULT)
+            pairs = weighted[:].rearrange("p (q i) -> p q i", i=PER_BRANCH)
+            branch_sum = sums.tile([P, BRANCHES], F32, name="branch_sum")
+            for i in range(PER_BRANCH):
+                nc.tensor.matmul(
+                    branch_sum[:], identity[:], pairs[:, :, i], start=(i == 0), stop=(i == PER_BRANCH - 1)
+                )
+            branch[s] = work.tile([P, BRANCHES], F32, name="branch")
+            nc.scalar.activation(branch[s][:], branch_sum[:], TANH)
+
+        def make_neurons(s):
+            b, k = divmod(s, PIECES)
+            grouped = work.tile([P, BRANCHES], F32, name="grouped")
+            nc.vector.tensor_tensor(grouped[:], branch[s][:], group_w[b][k][:], MULT)
+            quads = grouped[:].rearrange("p (n r) -> p n r", r=PER_GROUP)
+            group_sum = sums.tile([P, NEURONS], F32, name="group_sum")
+            for r in range(PER_GROUP):
+                nc.tensor.matmul(
+                    group_sum[:], identity[:], quads[:, :, r], start=(r == 0), stop=(r == PER_GROUP - 1)
+                )
+            nc.scalar.activation(result[b][:, k * NEURONS : (k + 1) * NEURONS], group_sum[:], TANH)
+            if k == PIECES - 1:
+                nc.sync.dma_start(out[b * P : (b + 1) * P, :], result[b][:])
+
+        make_gate(0)
+        make_gate(1)
+        make_weights(0)
+        for s in range(STEPS + BEHIND):
+            if s + 2 < PIECES:
+                make_gate(s + 2)
+            if s + 1 < STEPS:
+                make_weights(s + 1)
+            if s < STEPS:
+                make_branches(s)
+            if s >= BEHIND:
+                make_neurons(s - BEHIND)

@@ -20,7 +20,9 @@ PIECES = N // PIECE
 BRANCHES = PIECE // PER_BRANCH
 NEURONS = BRANCHES // PER_GROUP
 STEPS = BLOCKS * PIECES
+PER_SUM = 2
 BEHIND = 2
+SUMS = PIECES // PER_SUM
 
 
 def tile_memorygraph_kernel(tc, x, br_w, w_logit, grp_w, offs, out):
@@ -31,22 +33,28 @@ def tile_memorygraph_kernel(tc, x, br_w, w_logit, grp_w, offs, out):
         tc.psum_pool(name="sums", bufs=3) as sums,
     ):
         offsets = held.tile([P, N // 16], U16, name="offsets")
-        nc.sync.dma_start(offsets[:], offs)
-
         logit_rows = w_logit.rearrange("o n -> (o n)").partition_broadcast(P)
         windows, branch_w, group_w, logits = [], [], [], []
         for b in range(BLOCKS):
             rows = slice(b * P, (b + 1) * P)
-            windows.append(held.tile([P, S], F32, name=f"window{b}"))
-            nc.sync.dma_start(windows[b][:], x[rows, :])
             branch_w.append([held.tile([P, PIECE], F32, name=f"branch_w{b}_{k}") for k in range(PIECES)])
-            group_w.append([held.tile([P, BRANCHES], F32, name=f"group_w{b}_{k}") for k in range(PIECES)])
+            group_w.append([held.tile([P, PER_SUM * BRANCHES], F32, name=f"group_w{b}_{m}") for m in range(SUMS)])
             for k in range(PIECES):
+                entries = slice(k * PIECE, (k + 1) * PIECE)
                 if b == 0:
                     logits.append(held.tile([P, PIECE], F32, name=f"logits{k}"))
-                    nc.sync.dma_start(logits[k][:], logit_rows[:, k * PIECE : (k + 1) * PIECE])
-                nc.sync.dma_start(branch_w[b][k][:], br_w[rows, k * PIECE : (k + 1) * PIECE])
-                nc.sync.dma_start(group_w[b][k][:], grp_w[rows, k * BRANCHES : (k + 1) * BRANCHES])
+                    nc.sync.dma_start(logits[k][:], logit_rows[:, entries])
+                nc.sync.dma_start(branch_w[b][k][:], br_w[rows, entries])
+                if b == 0 and k == 0:
+                    nc.sync.dma_start(offsets[:], offs)
+                if k == 0:
+                    windows.append(held.tile([P, S], F32, name=f"window{b}"))
+                    nc.sync.dma_start(windows[b][:], x[rows, :])
+                if k % PER_SUM == 0:
+                    m = k // PER_SUM
+                    nc.sync.dma_start(
+                        group_w[b][m][:], grp_w[rows, m * PER_SUM * BRANCHES : (m + 1) * PER_SUM * BRANCHES]
+                    )
 
         identity = held.tile([P, P], F32, name="identity")
         make_identity(nc, identity[:])
@@ -74,32 +82,35 @@ def tile_memorygraph_kernel(tc, x, br_w, w_logit, grp_w, offs, out):
                 nc.tensor.matmul(
                     branch_sum[:], identity[:], pairs[:, :, i], start=(i == 0), stop=(i == PER_BRANCH - 1)
                 )
-            branch[s] = work.tile([P, BRANCHES], F32, name="branch")
-            nc.scalar.activation(branch[s][:], branch_sum[:], TANH)
+            g, h = divmod(s, PER_SUM)
+            if h == 0:
+                branch[g] = work.tile([P, PER_SUM * BRANCHES], F32, name="branch")
+            nc.scalar.activation(branch[g][:, h * BRANCHES : (h + 1) * BRANCHES], branch_sum[:], TANH)
 
-        def make_neurons(s):
-            b, k = divmod(s, PIECES)
-            grouped = work.tile([P, BRANCHES], F32, name="grouped")
-            nc.vector.tensor_tensor(grouped[:], branch[s][:], group_w[b][k][:], MULT)
+        def make_neurons(g):
+            b, m = divmod(g, SUMS)
+            grouped = work.tile([P, PER_SUM * BRANCHES], F32, name="grouped")
+            nc.vector.tensor_tensor(grouped[:], branch[g][:], group_w[b][m][:], MULT)
             quads = grouped[:].rearrange("p (n r) -> p n r", r=PER_GROUP)
-            group_sum = sums.tile([P, NEURONS], F32, name="group_sum")
+            group_sum = sums.tile([P, PER_SUM * NEURONS], F32, name="group_sum")
             for r in range(PER_GROUP):
                 nc.tensor.matmul(
                     group_sum[:], identity[:], quads[:, :, r], start=(r == 0), stop=(r == PER_GROUP - 1)
                 )
-            nc.scalar.activation(result[b][:, k * NEURONS : (k + 1) * NEURONS], group_sum[:], TANH)
-            if k == PIECES - 1:
+            nc.scalar.activation(
+                result[b][:, m * PER_SUM * NEURONS : (m + 1) * PER_SUM * NEURONS], group_sum[:], TANH
+            )
+            if m == SUMS - 1:
                 nc.sync.dma_start(out[b * P : (b + 1) * P, :], result[b][:])
 
         make_gate(0)
-        make_gate(1)
         make_weights(0)
         for s in range(STEPS + BEHIND):
-            if s + 2 < PIECES:
-                make_gate(s + 2)
-            if s + 1 < STEPS:
-                make_weights(s + 1)
+            if s + 1 < PIECES:
+                make_gate(s + 1)
             if s < STEPS:
                 make_branches(s)
-            if s >= BEHIND:
-                make_neurons(s - BEHIND)
+            if s + 1 < STEPS:
+                make_weights(s + 1)
+            if s >= BEHIND and (s - BEHIND) % PER_SUM == PER_SUM - 1:
+                make_neurons((s - BEHIND) // PER_SUM)

@@ -4,7 +4,6 @@ from concourse.masks import make_identity
 F32 = mybir.dt.float32
 U16 = mybir.dt.uint16
 MULT = mybir.AluOpType.mult
-ADD = mybir.AluOpType.add
 SIGMOID = mybir.ActivationFunctionType.Sigmoid
 TANH = mybir.ActivationFunctionType.Tanh
 
@@ -19,98 +18,88 @@ PIECE = S
 PIECES = N // PIECE
 BRANCHES = PIECE // PER_BRANCH
 NEURONS = BRANCHES // PER_GROUP
-STEPS = BLOCKS * PIECES
-PER_SUM = 2
-BEHIND = 2
-SUMS = PIECES // PER_SUM
+BEHIND = 1
 
 
 def tile_memorygraph_kernel(tc, x, br_w, w_logit, grp_w, offs, out):
     nc = tc.nc
     with (
         tc.tile_pool(name="held", bufs=1) as held,
-        tc.tile_pool(name="work", bufs=4) as work,
+        tc.tile_pool(name="work", bufs=3) as work,
         tc.psum_pool(name="sums", bufs=3) as sums,
     ):
+        br_w_blocks = br_w.rearrange("(b p) j -> p b j", p=P)
+        grp_w_blocks = grp_w.rearrange("(b p) q -> p b q", p=P)
+        out_blocks = out.rearrange("(b p) n -> p b n", p=P)
+        logit_rows = w_logit.rearrange("o j -> (o j)").partition_broadcast(P)
+
         offsets = held.tile([P, N // 16], U16, name="offsets")
-        logit_rows = w_logit.rearrange("o n -> (o n)").partition_broadcast(P)
-        windows, branch_w, group_w, logits = [], [], [], []
-        for b in range(BLOCKS):
-            rows = slice(b * P, (b + 1) * P)
-            branch_w.append([held.tile([P, PIECE], F32, name=f"branch_w{b}_{k}") for k in range(PIECES)])
-            group_w.append([held.tile([P, PER_SUM * BRANCHES], F32, name=f"group_w{b}_{m}") for m in range(SUMS)])
-            for k in range(PIECES):
-                entries = slice(k * PIECE, (k + 1) * PIECE)
-                if b == 0:
-                    logits.append(held.tile([P, PIECE], F32, name=f"logits{k}"))
-                    nc.sync.dma_start(logits[k][:], logit_rows[:, entries])
-                nc.sync.dma_start(branch_w[b][k][:], br_w[rows, entries])
-                if b == 0 and k == 0:
-                    nc.sync.dma_start(offsets[:], offs)
-                if k == 0:
-                    windows.append(held.tile([P, S], F32, name=f"window{b}"))
-                    nc.sync.dma_start(windows[b][:], x[rows, :])
-                if k % PER_SUM == 0:
-                    m = k // PER_SUM
-                    nc.sync.dma_start(
-                        group_w[b][m][:], grp_w[rows, m * PER_SUM * BRANCHES : (m + 1) * PER_SUM * BRANCHES]
-                    )
+        windows = [held.tile([P, S], F32, name=f"window{b}") for b in range(BLOCKS)]
+        logits = [held.tile([P, PIECE], F32, name=f"logits{k}") for k in range(PIECES)]
+        branch_w = [held.tile([P, BLOCKS, PIECE], F32, name=f"branch_w{k}") for k in range(PIECES)]
+        group_w = [held.tile([P, BLOCKS, BRANCHES], F32, name=f"group_w{k}") for k in range(PIECES)]
+        for k in range(PIECES):
+            nc.sync.dma_start(logits[k][:], logit_rows[:, k * PIECE : (k + 1) * PIECE])
+            nc.sync.dma_start(branch_w[k][:], br_w_blocks[:, :, k * PIECE : (k + 1) * PIECE])
+            if k == 0:
+                nc.sync.dma_start(offsets[:], offs)
+                for b in range(BLOCKS):
+                    nc.sync.dma_start(windows[b][:], x[b * P : (b + 1) * P, :])
+            nc.sync.dma_start(group_w[k][:], grp_w_blocks[:, :, k * BRANCHES : (k + 1) * BRANCHES])
 
         identity = held.tile([P, P], F32, name="identity")
         make_identity(nc, identity[:])
 
         gate = [held.tile([P, PIECE], F32, name=f"gate{k}") for k in range(PIECES)]
-        result = [held.tile([P, S], F32, name=f"result{b}") for b in range(BLOCKS)]
+        result = held.tile([P, BLOCKS, S], F32, name="result")
         weights, branch = {}, {}
 
         def make_gate(k):
             nc.scalar.activation(gate[k][:], logits[k][:], SIGMOID)
 
-        def make_weights(s):
-            b, k = divmod(s, PIECES)
-            weights[s] = work.tile([P, PIECE], F32, name="weights")
-            nc.vector.tensor_tensor(weights[s][:], branch_w[b][k][:], gate[k][:], MULT)
+        def make_weights(k):
+            weights[k] = work.tile([P, BLOCKS, PIECE], F32, name="weights")
+            both = gate[k][:].unsqueeze(1).to_broadcast([P, BLOCKS, PIECE])
+            nc.vector.tensor_tensor(weights[k][:], branch_w[k][:], both, MULT)
 
-        def make_branches(s):
-            b, k = divmod(s, PIECES)
-            picked = windows[b][:].indirect(offsets[:, k * (PIECE // 16) : (k + 1) * (PIECE // 16)])
-            weighted = work.tile([P, PIECE], F32, name="weighted")
-            nc.vector.tensor_tensor(weighted[:], picked, weights[s][:], MULT)
-            pairs = weighted[:].rearrange("p (q i) -> p q i", i=PER_BRANCH)
-            branch_sum = sums.tile([P, BRANCHES], F32, name="branch_sum")
-            for i in range(PER_BRANCH):
-                nc.tensor.matmul(
-                    branch_sum[:], identity[:], pairs[:, :, i], start=(i == 0), stop=(i == PER_BRANCH - 1)
-                )
-            g, h = divmod(s, PER_SUM)
-            if h == 0:
-                branch[g] = work.tile([P, PER_SUM * BRANCHES], F32, name="branch")
-            nc.scalar.activation(branch[g][:, h * BRANCHES : (h + 1) * BRANCHES], branch_sum[:], TANH)
+        def make_branches(k):
+            branch[k] = work.tile([P, BLOCKS, BRANCHES], F32, name="branch")
+            for b in range(BLOCKS):
+                picked = windows[b][:].indirect(offsets[:, k * (PIECE // 16) : (k + 1) * (PIECE // 16)])
+                weighted = work.tile([P, PIECE], F32, name="weighted")
+                nc.vector.tensor_tensor(weighted[:], picked, weights[k][:, b, :], MULT)
+                pairs = weighted[:].rearrange("p (q i) -> p q i", i=PER_BRANCH)
+                branch_sum = sums.tile([P, BRANCHES], F32, name="branch_sum")
+                for i in range(PER_BRANCH):
+                    nc.tensor.matmul(
+                        branch_sum[:], identity[:], pairs[:, :, i], start=(i == 0), stop=(i == PER_BRANCH - 1)
+                    )
+                nc.scalar.activation(branch[k][:, b, :], branch_sum[:], TANH)
 
-        def make_neurons(g):
-            b, m = divmod(g, SUMS)
-            grouped = work.tile([P, PER_SUM * BRANCHES], F32, name="grouped")
-            nc.vector.tensor_tensor(grouped[:], branch[g][:], group_w[b][m][:], MULT)
-            quads = grouped[:].rearrange("p (n r) -> p n r", r=PER_GROUP)
-            group_sum = sums.tile([P, PER_SUM * NEURONS], F32, name="group_sum")
+        def make_neurons(k):
+            grouped = work.tile([P, BLOCKS, BRANCHES], F32, name="grouped")
+            nc.vector.tensor_tensor(grouped[:], branch[k][:], group_w[k][:], MULT)
+            quads = grouped[:].rearrange("p b (n r) -> p (b n) r", r=PER_GROUP)
+            group_sum = sums.tile([P, BLOCKS, NEURONS], F32, name="group_sum")
             for r in range(PER_GROUP):
                 nc.tensor.matmul(
-                    group_sum[:], identity[:], quads[:, :, r], start=(r == 0), stop=(r == PER_GROUP - 1)
+                    group_sum[:].rearrange("p b n -> p (b n)"),
+                    identity[:],
+                    quads[:, :, r],
+                    start=(r == 0),
+                    stop=(r == PER_GROUP - 1),
                 )
-            nc.scalar.activation(
-                result[b][:, m * PER_SUM * NEURONS : (m + 1) * PER_SUM * NEURONS], group_sum[:], TANH
-            )
-            if m == SUMS - 1:
-                nc.sync.dma_start(out[b * P : (b + 1) * P, :], result[b][:])
+            nc.scalar.activation(result[:, :, k * NEURONS : (k + 1) * NEURONS], group_sum[:], TANH)
 
         make_gate(0)
         make_weights(0)
-        for s in range(STEPS + BEHIND):
-            if s + 1 < PIECES:
-                make_gate(s + 1)
-            if s < STEPS:
-                make_branches(s)
-            if s + 1 < STEPS:
-                make_weights(s + 1)
-            if s >= BEHIND and (s - BEHIND) % PER_SUM == PER_SUM - 1:
-                make_neurons((s - BEHIND) // PER_SUM)
+        for k in range(PIECES + BEHIND):
+            if k + 1 < PIECES:
+                make_gate(k + 1)
+            if k < PIECES:
+                make_branches(k)
+            if k + 1 < PIECES:
+                make_weights(k + 1)
+            if k >= BEHIND:
+                make_neurons(k - BEHIND)
+        nc.sync.dma_start(out_blocks, result[:])

@@ -4,6 +4,7 @@ from concourse.masks import make_identity
 F32 = mybir.dt.float32
 U16 = mybir.dt.uint16
 MULT = mybir.AluOpType.mult
+ADD = mybir.AluOpType.add
 SIGMOID = mybir.ActivationFunctionType.Sigmoid
 TANH = mybir.ActivationFunctionType.Tanh
 
@@ -50,8 +51,18 @@ def tile_memorygraph_kernel(tc, x, br_w, w_logit, grp_w, offs, out):
         identity = held.tile([P, P], F32, name="identity")
         make_identity(nc, identity[:])
 
+        def add_up(terms, name, by_vector):
+            columns, count = terms.shape[1], terms.shape[2]
+            if by_vector:
+                total = work.tile([P, columns], F32, name=name + "_by_vector")
+                nc.vector.tensor_reduce(total[:], terms, mybir.AxisListType.X, ADD)
+            else:
+                total = sums.tile([P, columns], F32, name=name)
+                for i in range(count):
+                    nc.tensor.matmul(total[:], identity[:], terms[:, :, i], start=(i == 0), stop=(i == count - 1))
+            return total
+
         gate = [held.tile([P, PIECE], F32, name=f"gate{k}") for k in range(PIECES)]
-        result = held.tile([P, BLOCKS, S], F32, name="result")
         weights, branch = {}, {}
 
         def make_gate(k):
@@ -69,27 +80,17 @@ def tile_memorygraph_kernel(tc, x, br_w, w_logit, grp_w, offs, out):
                 weighted = work.tile([P, PIECE], F32, name="weighted")
                 nc.vector.tensor_tensor(weighted[:], picked, weights[k][:, b, :], MULT)
                 pairs = weighted[:].rearrange("p (q i) -> p q i", i=PER_BRANCH)
-                branch_sum = sums.tile([P, BRANCHES], F32, name="branch_sum")
-                for i in range(PER_BRANCH):
-                    nc.tensor.matmul(
-                        branch_sum[:], identity[:], pairs[:, :, i], start=(i == 0), stop=(i == PER_BRANCH - 1)
-                    )
+                branch_sum = add_up(pairs, "branch_sum", by_vector=(k == PIECES - 1 and b == BLOCKS - 1))
                 nc.scalar.activation(branch[k][:, b, :], branch_sum[:], TANH)
 
         def make_neurons(k):
             grouped = work.tile([P, BLOCKS, BRANCHES], F32, name="grouped")
             nc.vector.tensor_tensor(grouped[:], branch[k][:], group_w[k][:], MULT)
             quads = grouped[:].rearrange("p b (n r) -> p (b n) r", r=PER_GROUP)
-            group_sum = sums.tile([P, BLOCKS, NEURONS], F32, name="group_sum")
-            for r in range(PER_GROUP):
-                nc.tensor.matmul(
-                    group_sum[:].rearrange("p b n -> p (b n)"),
-                    identity[:],
-                    quads[:, :, r],
-                    start=(r == 0),
-                    stop=(r == PER_GROUP - 1),
-                )
-            nc.scalar.activation(result[:, :, k * NEURONS : (k + 1) * NEURONS], group_sum[:], TANH)
+            group_sum = add_up(quads, "group_sum", by_vector=(k == PIECES - 1))
+            neurons = held.tile([P, BLOCKS, NEURONS], F32, name=f"neurons{k}")
+            nc.scalar.activation(neurons[:].rearrange("p b n -> p (b n)"), group_sum[:], TANH)
+            nc.sync.dma_start(out_blocks[:, :, k * NEURONS : (k + 1) * NEURONS], neurons[:])
 
         make_gate(0)
         make_weights(0)
@@ -102,4 +103,3 @@ def tile_memorygraph_kernel(tc, x, br_w, w_logit, grp_w, offs, out):
                 make_weights(k + 1)
             if k >= BEHIND:
                 make_neurons(k - BEHIND)
-        nc.sync.dma_start(out_blocks, result[:])

@@ -20,6 +20,7 @@ PIECES = N // PIECE
 BRANCHES = PIECE // PER_BRANCH
 NEURONS = BRANCHES // PER_GROUP
 BEHIND = 1
+BY_VECTOR = 3
 
 
 def tile_memorygraph_kernel(tc, x, br_w, w_logit, grp_w, offs, out):
@@ -87,7 +88,7 @@ def tile_memorygraph_kernel(tc, x, br_w, w_logit, grp_w, offs, out):
             grouped = work.tile([P, BLOCKS, BRANCHES], F32, name="grouped")
             nc.vector.tensor_tensor(grouped[:], branch[k][:], group_w[k][:], MULT)
             quads = grouped[:].rearrange("p b (n r) -> p (b n) r", r=PER_GROUP)
-            group_sum = add_up(quads, "group_sum", by_vector=(k == PIECES - 1))
+            group_sum = add_up(quads, "group_sum", by_vector=(k >= PIECES - BY_VECTOR))
             neurons = held.tile([P, BLOCKS, NEURONS], F32, name=f"neurons{k}")
             nc.scalar.activation(neurons[:].rearrange("p b n -> p (b n)"), group_sum[:], TANH)
             nc.sync.dma_start(out_blocks[:, :, k * NEURONS : (k + 1) * NEURONS], neurons[:])

@@ -5,8 +5,10 @@ F32 = mybir.dt.float32
 U16 = mybir.dt.uint16
 MULT = mybir.AluOpType.mult
 ADD = mybir.AluOpType.add
+ALONG_ROW = mybir.AxisListType.X
 SIGMOID = mybir.ActivationFunctionType.Sigmoid
 TANH = mybir.ActivationFunctionType.Tanh
+COPY = mybir.ActivationFunctionType.Copy
 
 P = 128
 C = 256
@@ -17,10 +19,13 @@ PER_GROUP = 4
 BLOCKS = C // P
 PIECE = S
 PIECES = N // PIECE
+UNITS = PIECES * BLOCKS
 BRANCHES = PIECE // PER_BRANCH
 NEURONS = BRANCHES // PER_GROUP
-BEHIND = 1
-BY_VECTOR = 3
+CHUNK = P
+CHUNKS = N // CHUNK
+CHUNKS_IN_PIECE = PIECE // CHUNK
+PAIRS = CHUNK // PER_BRANCH
 
 
 def tile_memorygraph_kernel(tc, x, br_w, w_logit, grp_w, offs, out):
@@ -28,79 +33,95 @@ def tile_memorygraph_kernel(tc, x, br_w, w_logit, grp_w, offs, out):
     with (
         tc.tile_pool(name="held", bufs=1) as held,
         tc.tile_pool(name="work", bufs=3) as work,
-        tc.psum_pool(name="sums", bufs=3) as sums,
+        tc.psum_pool(name="once", bufs=1) as once,
+        tc.psum_pool(name="flips", bufs=2) as flips,
+        tc.psum_pool(name="sums", bufs=2) as sums,
     ):
-        br_w_blocks = br_w.rearrange("(b p) j -> p b j", p=P)
         grp_w_blocks = grp_w.rearrange("(b p) q -> p b q", p=P)
         out_blocks = out.rearrange("(b p) n -> p b n", p=P)
-        logit_rows = w_logit.rearrange("o j -> (o j)").partition_broadcast(P)
 
+        logit_rows = held.tile([CHUNKS, CHUNK], F32, name="logit_rows")
         offsets = held.tile([P, N // 16], U16, name="offsets")
         windows = [held.tile([P, S], F32, name=f"window{b}") for b in range(BLOCKS)]
-        logits = [held.tile([P, PIECE], F32, name=f"logits{k}") for k in range(PIECES)]
-        branch_w = [held.tile([P, BLOCKS, PIECE], F32, name=f"branch_w{k}") for k in range(PIECES)]
+        branch_w = [held.tile([P, PIECE], F32, name=f"branch_w{u}") for u in range(UNITS)]
         group_w = [held.tile([P, BLOCKS, BRANCHES], F32, name=f"group_w{k}") for k in range(PIECES)]
+        nc.sync.dma_start(logit_rows[:], w_logit.rearrange("o (a j) -> (o a) j", j=CHUNK))
+        nc.sync.dma_start(offsets[:], offs)
         for k in range(PIECES):
-            nc.sync.dma_start(logits[k][:], logit_rows[:, k * PIECE : (k + 1) * PIECE])
-            nc.sync.dma_start(branch_w[k][:], br_w_blocks[:, :, k * PIECE : (k + 1) * PIECE])
-            if k == 0:
-                nc.sync.dma_start(offsets[:], offs)
-                for b in range(BLOCKS):
+            for b in range(BLOCKS):
+                if k == 0:
                     nc.sync.dma_start(windows[b][:], x[b * P : (b + 1) * P, :])
+                nc.sync.dma_start(
+                    branch_w[k * BLOCKS + b][:], br_w[b * P : (b + 1) * P, k * PIECE : (k + 1) * PIECE]
+                )
             nc.sync.dma_start(group_w[k][:], grp_w_blocks[:, :, k * BRANCHES : (k + 1) * BRANCHES])
 
         identity = held.tile([P, P], F32, name="identity")
         make_identity(nc, identity[:])
+        pair_of = held.tile([P, PAIRS], F32, name="pair_of")
+        nc.vector.tensor_reduce(
+            pair_of[:], identity[:].rearrange("p (q i) -> p q i", i=PER_BRANCH), ALONG_ROW, ADD
+        )
 
-        def add_up(terms, name, by_vector):
-            columns, count = terms.shape[1], terms.shape[2]
-            if by_vector:
-                total = work.tile([P, columns], F32, name=name + "_by_vector")
-                nc.vector.tensor_reduce(total[:], terms, mybir.AxisListType.X, ADD)
-            else:
-                total = sums.tile([P, columns], F32, name=name)
-                for i in range(count):
-                    nc.tensor.matmul(total[:], identity[:], terms[:, :, i], start=(i == 0), stop=(i == count - 1))
-            return total
+        logit_columns = once.tile([P, CHUNKS], F32, name="logit_columns")
+        nc.tensor.matmul(logit_columns[:], logit_rows[:], identity[0:CHUNKS, 0:CHUNKS], start=True, stop=True)
+        gate = held.tile([P, CHUNKS], F32, name="gate")
+        nc.scalar.activation(gate[:], logit_columns[:], SIGMOID)
 
-        gate = [held.tile([P, PIECE], F32, name=f"gate{k}") for k in range(PIECES)]
-        weights, branch = {}, {}
+        gated_pair_of, product, flipped, branch = {}, {}, {}, {}
 
-        def make_gate(k):
-            nc.scalar.activation(gate[k][:], logits[k][:], SIGMOID)
+        def make_gated_pairs(k):
+            gated_pair_of[k] = held.tile([P, CHUNKS_IN_PIECE, PAIRS], F32, name=f"gated_pair_of{k}")
+            for a in range(CHUNKS_IN_PIECE):
+                chunk = k * CHUNKS_IN_PIECE + a
+                nc.scalar.activation(gated_pair_of[k][:, a, :], pair_of[:], COPY, scale=gate[:, chunk : chunk + 1])
 
-        def make_weights(k):
-            weights[k] = work.tile([P, BLOCKS, PIECE], F32, name="weights")
-            both = gate[k][:].unsqueeze(1).to_broadcast([P, BLOCKS, PIECE])
-            nc.vector.tensor_tensor(weights[k][:], branch_w[k][:], both, MULT)
+        def look_up(u):
+            k, b = divmod(u, BLOCKS)
+            picked = windows[b][:].indirect(offsets[:, k * (PIECE // 16) : (k + 1) * (PIECE // 16)])
+            product[u] = work.tile([P, PIECE], F32, name="product")
+            nc.vector.tensor_tensor(product[u][:], picked, branch_w[u][:], MULT)
 
-        def make_branches(k):
-            branch[k] = work.tile([P, BLOCKS, BRANCHES], F32, name="branch")
-            for b in range(BLOCKS):
-                picked = windows[b][:].indirect(offsets[:, k * (PIECE // 16) : (k + 1) * (PIECE // 16)])
-                weighted = work.tile([P, PIECE], F32, name="weighted")
-                nc.vector.tensor_tensor(weighted[:], picked, weights[k][:, b, :], MULT)
-                pairs = weighted[:].rearrange("p (q i) -> p q i", i=PER_BRANCH)
-                branch_sum = add_up(pairs, "branch_sum", by_vector=(k == PIECES - 1 and b == BLOCKS - 1))
-                nc.scalar.activation(branch[k][:, b, :], branch_sum[:], TANH)
+        def flip(u):
+            flipped_in_psum = flips.tile([P, CHUNKS_IN_PIECE, P], F32, name="flipped_in_psum")
+            for a in range(CHUNKS_IN_PIECE):
+                nc.tensor.transpose(flipped_in_psum[:, a, :], product[u][:, a * CHUNK : (a + 1) * CHUNK], identity[:])
+            flipped[u] = work.tile([P, CHUNKS_IN_PIECE, P], F32, name="flipped")
+            nc.scalar.copy(flipped[u][:], flipped_in_psum[:])
+
+        def make_branches(u):
+            k, b = divmod(u, BLOCKS)
+            if b == 0:
+                branch[k] = work.tile([P, BLOCKS, BRANCHES], F32, name="branch")
+            branch_sum = sums.tile([P, BRANCHES], F32, name="branch_sum")
+            for a in range(CHUNKS_IN_PIECE):
+                nc.tensor.matmul(
+                    branch_sum[:, a * PAIRS : (a + 1) * PAIRS],
+                    flipped[u][:, a, :],
+                    gated_pair_of[k][:, a, :],
+                    start=True,
+                    stop=True,
+                )
+            nc.scalar.activation(branch[k][:, b, :], branch_sum[:], TANH)
 
         def make_neurons(k):
             grouped = work.tile([P, BLOCKS, BRANCHES], F32, name="grouped")
             nc.vector.tensor_tensor(grouped[:], branch[k][:], group_w[k][:], MULT)
+            group_sum = work.tile([P, BLOCKS * NEURONS], F32, name="group_sum")
             quads = grouped[:].rearrange("p b (n r) -> p (b n) r", r=PER_GROUP)
-            group_sum = add_up(quads, "group_sum", by_vector=(k >= PIECES - BY_VECTOR))
+            nc.vector.tensor_reduce(group_sum[:], quads, ALONG_ROW, ADD)
             neurons = held.tile([P, BLOCKS, NEURONS], F32, name=f"neurons{k}")
             nc.scalar.activation(neurons[:].rearrange("p b n -> p (b n)"), group_sum[:], TANH)
             nc.sync.dma_start(out_blocks[:, :, k * NEURONS : (k + 1) * NEURONS], neurons[:])
 
-        make_gate(0)
-        make_weights(0)
-        for k in range(PIECES + BEHIND):
-            if k + 1 < PIECES:
-                make_gate(k + 1)
-            if k < PIECES:
-                make_branches(k)
-            if k + 1 < PIECES:
-                make_weights(k + 1)
-            if k >= BEHIND:
-                make_neurons(k - BEHIND)
+        make_gated_pairs(0)
+        for u in range(UNITS + 3):
+            if u < UNITS:
+                look_up(u)
+                flip(u)
+            if u % BLOCKS == 0 and u // BLOCKS + 1 < PIECES:
+                make_gated_pairs(u // BLOCKS + 1)
+            if 1 <= u <= UNITS:
+                make_branches(u - 1)
+            if u >= 3 and u % BLOCKS == 1:
+                make_neurons((u - 3) // BLOCKS)

@@ -22,10 +22,11 @@ PIECES = N // PIECE
 UNITS = PIECES * BLOCKS
 BRANCHES = PIECE // PER_BRANCH
 NEURONS = BRANCHES // PER_GROUP
-CHUNK = P
-CHUNKS = N // CHUNK
-CHUNKS_IN_PIECE = PIECE // CHUNK
-PAIRS = CHUNK // PER_BRANCH
+SLAB = P * PER_BRANCH
+SLABS = N // SLAB
+SLABS_IN_PIECE = PIECE // SLAB
+LOADED = 2
+BEHIND = 3
 
 
 def tile_memorygraph_kernel(tc, x, br_w, w_logit, grp_w, offs, out):
@@ -40,73 +41,82 @@ def tile_memorygraph_kernel(tc, x, br_w, w_logit, grp_w, offs, out):
         grp_w_blocks = grp_w.rearrange("(b p) q -> p b q", p=P)
         out_blocks = out.rearrange("(b p) n -> p b n", p=P)
 
-        logit_rows = held.tile([CHUNKS, CHUNK], F32, name="logit_rows")
+        logit_rows = held.tile([SLABS, SLAB], F32, name="logit_rows")
         offsets = held.tile([P, N // 16], U16, name="offsets")
         windows = [held.tile([P, S], F32, name=f"window{b}") for b in range(BLOCKS)]
-        branch_w = [held.tile([P, PIECE], F32, name=f"branch_w{u}") for u in range(UNITS)]
-        group_w = [held.tile([P, BLOCKS, BRANCHES], F32, name=f"group_w{k}") for k in range(PIECES)]
-        nc.sync.dma_start(logit_rows[:], w_logit.rearrange("o (a j) -> (o a) j", j=CHUNK))
+        branch_w = [
+            [held.tile([P, LOADED * PIECE], F32, name=f"branch_w{g}_{b}") for b in range(BLOCKS)]
+            for g in range(PIECES // LOADED)
+        ]
+        group_w = [held.tile([P, BLOCKS, LOADED * BRANCHES], F32, name=f"group_w{g}") for g in range(PIECES // LOADED)]
+        nc.sync.dma_start(logit_rows[:], w_logit.rearrange("o (m j) -> (o m) j", j=SLAB))
         nc.sync.dma_start(offsets[:], offs)
-        for k in range(PIECES):
+        for g in range(PIECES // LOADED):
             for b in range(BLOCKS):
-                if k == 0:
+                if g == 0:
                     nc.sync.dma_start(windows[b][:], x[b * P : (b + 1) * P, :])
                 nc.sync.dma_start(
-                    branch_w[k * BLOCKS + b][:], br_w[b * P : (b + 1) * P, k * PIECE : (k + 1) * PIECE]
+                    branch_w[g][b][:], br_w[b * P : (b + 1) * P, g * LOADED * PIECE : (g + 1) * LOADED * PIECE]
                 )
-            nc.sync.dma_start(group_w[k][:], grp_w_blocks[:, :, k * BRANCHES : (k + 1) * BRANCHES])
+            nc.sync.dma_start(
+                group_w[g][:], grp_w_blocks[:, :, g * LOADED * BRANCHES : (g + 1) * LOADED * BRANCHES]
+            )
 
         identity = held.tile([P, P], F32, name="identity")
         make_identity(nc, identity[:])
-        pair_of = held.tile([P, PAIRS], F32, name="pair_of")
-        nc.vector.tensor_reduce(
-            pair_of[:], identity[:].rearrange("p (q i) -> p q i", i=PER_BRANCH), ALONG_ROW, ADD
-        )
 
-        logit_columns = once.tile([P, CHUNKS], F32, name="logit_columns")
-        nc.tensor.matmul(logit_columns[:], logit_rows[:], identity[0:CHUNKS, 0:CHUNKS], start=True, stop=True)
-        gate = held.tile([P, CHUNKS], F32, name="gate")
+        logit_columns = once.tile([P, PER_BRANCH, SLABS], F32, name="logit_columns")
+        connections = logit_rows[:].rearrange("m (q i) -> m q i", i=PER_BRANCH)
+        for i in range(PER_BRANCH):
+            nc.tensor.matmul(
+                logit_columns[:, i, :], connections[:, :, i], identity[0:SLABS, 0:SLABS], start=True, stop=True
+            )
+        gate = held.tile([P, PER_BRANCH, SLABS], F32, name="gate")
         nc.scalar.activation(gate[:], logit_columns[:], SIGMOID)
 
-        gated_pair_of, product, flipped, branch = {}, {}, {}, {}
-
-        def make_gated_pairs(k):
-            gated_pair_of[k] = held.tile([P, CHUNKS_IN_PIECE, PAIRS], F32, name=f"gated_pair_of{k}")
-            for a in range(CHUNKS_IN_PIECE):
-                chunk = k * CHUNKS_IN_PIECE + a
-                nc.scalar.activation(gated_pair_of[k][:, a, :], pair_of[:], COPY, scale=gate[:, chunk : chunk + 1])
+        product, gated, branch = {}, {}, {}
 
         def look_up(u):
             k, b = divmod(u, BLOCKS)
             picked = windows[b][:].indirect(offsets[:, k * (PIECE // 16) : (k + 1) * (PIECE // 16)])
             product[u] = work.tile([P, PIECE], F32, name="product")
-            nc.vector.tensor_tensor(product[u][:], picked, branch_w[u][:], MULT)
+            g, i = divmod(k, LOADED)
+            nc.vector.tensor_tensor(product[u][:], picked, branch_w[g][b][:, i * PIECE : (i + 1) * PIECE], MULT)
 
-        def flip(u):
-            flipped_in_psum = flips.tile([P, CHUNKS_IN_PIECE, P], F32, name="flipped_in_psum")
-            for a in range(CHUNKS_IN_PIECE):
-                nc.tensor.transpose(flipped_in_psum[:, a, :], product[u][:, a * CHUNK : (a + 1) * CHUNK], identity[:])
-            flipped[u] = work.tile([P, CHUNKS_IN_PIECE, P], F32, name="flipped")
-            nc.scalar.copy(flipped[u][:], flipped_in_psum[:])
+        def flip_and_gate(u):
+            k = u // BLOCKS
+            by_connection = product[u][:].rearrange("p (h q i) -> p h q i", h=SLABS_IN_PIECE, i=PER_BRANCH)
+            flipped = flips.tile([P, SLABS_IN_PIECE, PER_BRANCH, P], F32, name="flipped")
+            for h in range(SLABS_IN_PIECE):
+                for i in range(PER_BRANCH):
+                    nc.tensor.transpose(flipped[:, h, i, :], by_connection[:, h, :, i], identity[:])
+            gated[u] = work.tile([P, SLABS_IN_PIECE, PER_BRANCH, P], F32, name="gated")
+            for h in range(SLABS_IN_PIECE):
+                m = k * SLABS_IN_PIECE + h
+                for i in range(PER_BRANCH):
+                    nc.scalar.activation(gated[u][:, h, i, :], flipped[:, h, i, :], COPY, scale=gate[:, i, m : m + 1])
 
         def make_branches(u):
             k, b = divmod(u, BLOCKS)
             if b == 0:
                 branch[k] = work.tile([P, BLOCKS, BRANCHES], F32, name="branch")
             branch_sum = sums.tile([P, BRANCHES], F32, name="branch_sum")
-            for a in range(CHUNKS_IN_PIECE):
-                nc.tensor.matmul(
-                    branch_sum[:, a * PAIRS : (a + 1) * PAIRS],
-                    flipped[u][:, a, :],
-                    gated_pair_of[k][:, a, :],
-                    start=True,
-                    stop=True,
-                )
+            for h in range(SLABS_IN_PIECE):
+                for i in range(PER_BRANCH):
+                    nc.tensor.matmul(
+                        branch_sum[:, h * P : (h + 1) * P],
+                        gated[u][:, h, i, :],
+                        identity[:],
+                        is_transpose=True,
+                        start=(i == 0),
+                        stop=(i == PER_BRANCH - 1),
+                    )
             nc.scalar.activation(branch[k][:, b, :], branch_sum[:], TANH)
 
         def make_neurons(k):
             grouped = work.tile([P, BLOCKS, BRANCHES], F32, name="grouped")
-            nc.vector.tensor_tensor(grouped[:], branch[k][:], group_w[k][:], MULT)
+            g, i = divmod(k, LOADED)
+            nc.vector.tensor_tensor(grouped[:], branch[k][:], group_w[g][:, :, i * BRANCHES : (i + 1) * BRANCHES], MULT)
             group_sum = work.tile([P, BLOCKS * NEURONS], F32, name="group_sum")
             quads = grouped[:].rearrange("p b (n r) -> p (b n) r", r=PER_GROUP)
             nc.vector.tensor_reduce(group_sum[:], quads, ALONG_ROW, ADD)
@@ -114,14 +124,11 @@ def tile_memorygraph_kernel(tc, x, br_w, w_logit, grp_w, offs, out):
             nc.scalar.activation(neurons[:].rearrange("p b n -> p (b n)"), group_sum[:], TANH)
             nc.sync.dma_start(out_blocks[:, :, k * NEURONS : (k + 1) * NEURONS], neurons[:])
 
-        make_gated_pairs(0)
-        for u in range(UNITS + 3):
+        for u in range(UNITS + BEHIND):
             if u < UNITS:
                 look_up(u)
-                flip(u)
-            if u % BLOCKS == 0 and u // BLOCKS + 1 < PIECES:
-                make_gated_pairs(u // BLOCKS + 1)
+                flip_and_gate(u)
             if 1 <= u <= UNITS:
                 make_branches(u - 1)
-            if u >= 3 and u % BLOCKS == 1:
-                make_neurons((u - 3) // BLOCKS)
+            if u > BEHIND and (u - BEHIND) % BLOCKS == 1:
+                make_neurons((u - BEHIND) // BLOCKS)

@@ -37,6 +37,7 @@ def tile_memorygraph_kernel(tc, x, br_w, w_logit, grp_w, offs, out):
         tc.psum_pool(name="once", bufs=1) as once,
         tc.psum_pool(name="flips", bufs=2) as flips,
         tc.psum_pool(name="sums", bufs=2) as sums,
+        tc.psum_pool(name="groups", bufs=1) as groups,
     ):
         grp_w_blocks = grp_w.rearrange("(b p) q -> p b q", p=P)
         out_blocks = out.rearrange("(b p) n -> p b n", p=P)
@@ -117,11 +118,29 @@ def tile_memorygraph_kernel(tc, x, br_w, w_logit, grp_w, offs, out):
             grouped = work.tile([P, BLOCKS, BRANCHES], F32, name="grouped")
             g, i = divmod(k, LOADED)
             nc.vector.tensor_tensor(grouped[:], branch[k][:], group_w[g][:, :, i * BRANCHES : (i + 1) * BRANCHES], MULT)
-            group_sum = work.tile([P, BLOCKS * NEURONS], F32, name="group_sum")
             quads = grouped[:].rearrange("p b (n r) -> p (b n) r", r=PER_GROUP)
-            nc.vector.tensor_reduce(group_sum[:], quads, ALONG_ROW, ADD)
             neurons = held.tile([P, BLOCKS, NEURONS], F32, name=f"neurons{k}")
-            nc.scalar.activation(neurons[:].rearrange("p b n -> p (b n)"), group_sum[:], TANH)
+            neurons_in_a_row = neurons[:].rearrange("p b n -> p (b n)")
+            if k == PIECES - 1:
+                group_sum = work.tile([P, BLOCKS * NEURONS], F32, name="group_sum")
+                nc.vector.tensor_reduce(group_sum[:], quads, ALONG_ROW, ADD)
+                nc.scalar.activation(neurons_in_a_row, group_sum[:], TANH)
+            else:
+                flipped_sum = groups.tile([BLOCKS * NEURONS, P], F32, name="flipped_sum")
+                for r in range(PER_GROUP):
+                    nc.tensor.matmul(
+                        flipped_sum[:],
+                        quads[:, :, r],
+                        identity[:],
+                        is_transpose=True,
+                        start=(r == 0),
+                        stop=(r == PER_GROUP - 1),
+                    )
+                flipped_neurons = work.tile([BLOCKS * NEURONS, P], F32, name="flipped_neurons")
+                nc.scalar.activation(flipped_neurons[:], flipped_sum[:], TANH)
+                neurons_in_psum = groups.tile([P, BLOCKS * NEURONS], F32, name="neurons_in_psum")
+                nc.tensor.transpose(neurons_in_psum[:], flipped_neurons[:], identity[:])
+                nc.scalar.copy(neurons_in_a_row, neurons_in_psum[:])
             nc.sync.dma_start(out_blocks[:, :, k * NEURONS : (k + 1) * NEURONS], neurons[:])
 
         for u in range(UNITS + BEHIND):

@@ -25,8 +25,15 @@ NEURONS = BRANCHES // PER_GROUP
 SLAB = P * PER_BRANCH
 SLABS = N // SLAB
 SLABS_IN_PIECE = PIECE // SLAB
-LOADED = 2
+LOAD_FROM = [0, 1, 2, 4]
+LOAD_PIECES = [1, 1, 2, 4]
+assert all(LOAD_FROM[g] == sum(LOAD_PIECES[:g]) for g in range(len(LOAD_FROM))) and sum(LOAD_PIECES) == PIECES
 BEHIND = 3
+
+
+def load_of(k):
+    g = max(g for g in range(len(LOAD_FROM)) if LOAD_FROM[g] <= k)
+    return g, k - LOAD_FROM[g]
 
 
 def tile_memorygraph_kernel(tc, x, br_w, w_logit, grp_w, offs, out):
@@ -46,22 +53,22 @@ def tile_memorygraph_kernel(tc, x, br_w, w_logit, grp_w, offs, out):
         offsets = held.tile([P, N // 16], U16, name="offsets")
         windows = [held.tile([P, S], F32, name=f"window{b}") for b in range(BLOCKS)]
         branch_w = [
-            [held.tile([P, LOADED * PIECE], F32, name=f"branch_w{g}_{b}") for b in range(BLOCKS)]
-            for g in range(PIECES // LOADED)
+            [held.tile([P, pieces * PIECE], F32, name=f"branch_w{g}_{b}") for b in range(BLOCKS)]
+            for g, pieces in enumerate(LOAD_PIECES)
         ]
-        group_w = [held.tile([P, BLOCKS, LOADED * BRANCHES], F32, name=f"group_w{g}") for g in range(PIECES // LOADED)]
+        group_w = [
+            held.tile([P, BLOCKS, pieces * BRANCHES], F32, name=f"group_w{g}") for g, pieces in enumerate(LOAD_PIECES)
+        ]
         nc.sync.dma_start(logit_rows[:], w_logit.rearrange("o (m j) -> (o m) j", j=SLAB))
         nc.sync.dma_start(offsets[:], offs)
-        for g in range(PIECES // LOADED):
+        for g, (first, pieces) in enumerate(zip(LOAD_FROM, LOAD_PIECES)):
             for b in range(BLOCKS):
                 if g == 0:
                     nc.sync.dma_start(windows[b][:], x[b * P : (b + 1) * P, :])
                 nc.sync.dma_start(
-                    branch_w[g][b][:], br_w[b * P : (b + 1) * P, g * LOADED * PIECE : (g + 1) * LOADED * PIECE]
+                    branch_w[g][b][:], br_w[b * P : (b + 1) * P, first * PIECE : (first + pieces) * PIECE]
                 )
-            nc.sync.dma_start(
-                group_w[g][:], grp_w_blocks[:, :, g * LOADED * BRANCHES : (g + 1) * LOADED * BRANCHES]
-            )
+            nc.sync.dma_start(group_w[g][:], grp_w_blocks[:, :, first * BRANCHES : (first + pieces) * BRANCHES])
 
         identity = held.tile([P, P], F32, name="identity")
         make_identity(nc, identity[:])
@@ -81,7 +88,7 @@ def tile_memorygraph_kernel(tc, x, br_w, w_logit, grp_w, offs, out):
             k, b = divmod(u, BLOCKS)
             picked = windows[b][:].indirect(offsets[:, k * (PIECE // 16) : (k + 1) * (PIECE // 16)])
             product[u] = work.tile([P, PIECE], F32, name="product")
-            g, i = divmod(k, LOADED)
+            g, i = load_of(k)
             nc.vector.tensor_tensor(product[u][:], picked, branch_w[g][b][:, i * PIECE : (i + 1) * PIECE], MULT)
 
         def flip_and_gate(u):
@@ -116,7 +123,7 @@ def tile_memorygraph_kernel(tc, x, br_w, w_logit, grp_w, offs, out):
 
         def make_neurons(k):
             grouped = work.tile([P, BLOCKS, BRANCHES], F32, name="grouped")
-            g, i = divmod(k, LOADED)
+            g, i = load_of(k)
             nc.vector.tensor_tensor(grouped[:], branch[k][:], group_w[g][:, :, i * BRANCHES : (i + 1) * BRANCHES], MULT)
             quads = grouped[:].rearrange("p b (n r) -> p (b n) r", r=PER_GROUP)
             neurons = held.tile([P, BLOCKS, NEURONS], F32, name=f"neurons{k}")

@@ -41,8 +41,8 @@ def tile_memorygraph_kernel(tc, x, br_w, w_logit, grp_w, offs, out):
     with (
         tc.tile_pool(name="held", bufs=1) as held,
         tc.tile_pool(name="work", bufs=3) as work,
-        tc.psum_pool(name="once", bufs=1) as once,
-        tc.psum_pool(name="flips", bufs=2) as flips,
+        tc.tile_pool(name="products", bufs=2) as products,
+        tc.psum_pool(name="flips", bufs=2 * SLABS_IN_PIECE) as flips,
         tc.psum_pool(name="sums", bufs=2) as sums,
         tc.psum_pool(name="groups", bufs=1) as groups,
     ):
@@ -73,7 +73,7 @@ def tile_memorygraph_kernel(tc, x, br_w, w_logit, grp_w, offs, out):
         identity = held.tile([P, P], F32, name="identity")
         make_identity(nc, identity[:])
 
-        logit_columns = once.tile([P, PER_BRANCH, SLABS], F32, name="logit_columns")
+        logit_columns = groups.tile([P, PER_BRANCH, SLABS], F32, name="logit_columns", tag="flipped_sum")
         connections = logit_rows[:].rearrange("m (q i) -> m q i", i=PER_BRANCH)
         for i in range(PER_BRANCH):
             nc.tensor.matmul(
@@ -87,22 +87,21 @@ def tile_memorygraph_kernel(tc, x, br_w, w_logit, grp_w, offs, out):
         def look_up(u):
             k, b = divmod(u, BLOCKS)
             picked = windows[b][:].indirect(offsets[:, k * (PIECE // 16) : (k + 1) * (PIECE // 16)])
-            product[u] = work.tile([P, PIECE], F32, name="product")
+            product[u] = products.tile([P, PIECE], F32, name="product")
             g, i = load_of(k)
             nc.vector.tensor_tensor(product[u][:], picked, branch_w[g][b][:, i * PIECE : (i + 1) * PIECE], MULT)
 
         def flip_and_gate(u):
             k = u // BLOCKS
             by_connection = product[u][:].rearrange("p (h q i) -> p h q i", h=SLABS_IN_PIECE, i=PER_BRANCH)
-            flipped = flips.tile([P, SLABS_IN_PIECE, PER_BRANCH, P], F32, name="flipped")
-            for h in range(SLABS_IN_PIECE):
-                for i in range(PER_BRANCH):
-                    nc.tensor.transpose(flipped[:, h, i, :], by_connection[:, h, :, i], identity[:])
             gated[u] = work.tile([P, SLABS_IN_PIECE, PER_BRANCH, P], F32, name="gated")
             for h in range(SLABS_IN_PIECE):
                 m = k * SLABS_IN_PIECE + h
+                flipped = flips.tile([P, PER_BRANCH, P], F32, name="flipped")
                 for i in range(PER_BRANCH):
-                    nc.scalar.activation(gated[u][:, h, i, :], flipped[:, h, i, :], COPY, scale=gate[:, i, m : m + 1])
+                    nc.tensor.transpose(flipped[:, i, :], by_connection[:, h, :, i], identity[:])
+                for i in range(PER_BRANCH):
+                    nc.scalar.activation(gated[u][:, h, i, :], flipped[:, i, :], COPY, scale=gate[:, i, m : m + 1])
 
         def make_branches(u):
             k, b = divmod(u, BLOCKS)
@@ -122,17 +121,20 @@ def tile_memorygraph_kernel(tc, x, br_w, w_logit, grp_w, offs, out):
             nc.scalar.activation(branch[k][:, b, :], branch_sum[:], TANH)
 
         def make_neurons(k):
-            grouped = work.tile([P, BLOCKS, BRANCHES], F32, name="grouped")
             g, i = load_of(k)
-            nc.vector.tensor_tensor(grouped[:], branch[k][:], group_w[g][:, :, i * BRANCHES : (i + 1) * BRANCHES], MULT)
-            quads = grouped[:].rearrange("p b (n r) -> p (b n) r", r=PER_GROUP)
+            weights = group_w[g][:, :, i * BRANCHES : (i + 1) * BRANCHES]
+            grouped = work.tile([P, BLOCKS, BRANCHES], F32, name="grouped")
             neurons = held.tile([P, BLOCKS, NEURONS], F32, name=f"neurons{k}")
-            neurons_in_a_row = neurons[:].rearrange("p b n -> p (b n)")
             if k == PIECES - 1:
-                group_sum = work.tile([P, BLOCKS * NEURONS], F32, name="group_sum")
-                nc.vector.tensor_reduce(group_sum[:], quads, ALONG_ROW, ADD)
-                nc.scalar.activation(neurons_in_a_row, group_sum[:], TANH)
+                group_sum = work.tile([P, BLOCKS, NEURONS], F32, name="group_sum")
+                for b in range(BLOCKS):
+                    nc.vector.tensor_tensor(grouped[:, b, :], branch[k][:, b, :], weights[:, b, :], MULT)
+                    quads = grouped[:, b, :].rearrange("p (n r) -> p n r", r=PER_GROUP)
+                    nc.vector.tensor_reduce(group_sum[:, b, :], quads, ALONG_ROW, ADD)
+                    nc.scalar.activation(neurons[:, b, :], group_sum[:, b, :], TANH)
             else:
+                nc.vector.tensor_tensor(grouped[:], branch[k][:], weights, MULT)
+                quads = grouped[:].rearrange("p b (n r) -> p (b n) r", r=PER_GROUP)
                 flipped_sum = groups.tile([BLOCKS * NEURONS, P], F32, name="flipped_sum")
                 for r in range(PER_GROUP):
                     nc.tensor.matmul(
@@ -147,7 +149,7 @@ def tile_memorygraph_kernel(tc, x, br_w, w_logit, grp_w, offs, out):
                 nc.scalar.activation(flipped_neurons[:], flipped_sum[:], TANH)
                 neurons_in_psum = groups.tile([P, BLOCKS * NEURONS], F32, name="neurons_in_psum")
                 nc.tensor.transpose(neurons_in_psum[:], flipped_neurons[:], identity[:])
-                nc.scalar.copy(neurons_in_a_row, neurons_in_psum[:])
+                nc.scalar.copy(neurons[:].rearrange("p b n -> p (b n)"), neurons_in_psum[:])
             nc.sync.dma_start(out_blocks[:, :, k * NEURONS : (k + 1) * NEURONS], neurons[:])
 
         for u in range(UNITS + BEHIND):

@@ -44,7 +44,7 @@ def tile_memorygraph_kernel(tc, x, br_w, w_logit, grp_w, offs, out):
         tc.tile_pool(name="products", bufs=2) as products,
         tc.psum_pool(name="flips", bufs=2 * SLABS_IN_PIECE) as flips,
         tc.psum_pool(name="sums", bufs=2) as sums,
-        tc.psum_pool(name="groups", bufs=1) as groups,
+        tc.psum_pool(name="groups", bufs=2) as groups,
     ):
         grp_w_blocks = grp_w.rearrange("(b p) q -> p b q", p=P)
         out_blocks = out.rearrange("(b p) n -> p b n", p=P)
@@ -73,7 +73,7 @@ def tile_memorygraph_kernel(tc, x, br_w, w_logit, grp_w, offs, out):
         identity = held.tile([P, P], F32, name="identity")
         make_identity(nc, identity[:])
 
-        logit_columns = groups.tile([P, PER_BRANCH, SLABS], F32, name="logit_columns", tag="flipped_sum")
+        logit_columns = groups.tile([P, PER_BRANCH, SLABS], F32, name="logit_columns", tag="sum_in_psum")
         connections = logit_rows[:].rearrange("m (q i) -> m q i", i=PER_BRANCH)
         for i in range(PER_BRANCH):
             nc.tensor.matmul(
@@ -123,9 +123,9 @@ def tile_memorygraph_kernel(tc, x, br_w, w_logit, grp_w, offs, out):
         def make_neurons(k):
             g, i = load_of(k)
             weights = group_w[g][:, :, i * BRANCHES : (i + 1) * BRANCHES]
-            grouped = work.tile([P, BLOCKS, BRANCHES], F32, name="grouped")
             neurons = held.tile([P, BLOCKS, NEURONS], F32, name=f"neurons{k}")
             if k == PIECES - 1:
+                grouped = work.tile([P, BLOCKS, BRANCHES], F32, name="grouped")
                 group_sum = work.tile([P, BLOCKS, NEURONS], F32, name="group_sum")
                 for b in range(BLOCKS):
                     nc.vector.tensor_tensor(grouped[:, b, :], branch[k][:, b, :], weights[:, b, :], MULT)
@@ -133,23 +133,19 @@ def tile_memorygraph_kernel(tc, x, br_w, w_logit, grp_w, offs, out):
                     nc.vector.tensor_reduce(group_sum[:, b, :], quads, ALONG_ROW, ADD)
                     nc.scalar.activation(neurons[:, b, :], group_sum[:, b, :], TANH)
             else:
-                nc.vector.tensor_tensor(grouped[:], branch[k][:], weights, MULT)
-                quads = grouped[:].rearrange("p b (n r) -> p (b n) r", r=PER_GROUP)
-                flipped_sum = groups.tile([BLOCKS * NEURONS, P], F32, name="flipped_sum")
+                apart = work.tile([P, PER_GROUP, BLOCKS * NEURONS], F32, name="apart")
+                nc.vector.tensor_tensor(
+                    apart[:].rearrange("p r (b n) -> p b n r", b=BLOCKS),
+                    branch[k][:].rearrange("p b (n r) -> p b n r", r=PER_GROUP),
+                    weights.rearrange("p b (n r) -> p b n r", r=PER_GROUP),
+                    MULT,
+                )
+                sum_in_psum = groups.tile([P, BLOCKS * NEURONS], F32, name="sum_in_psum")
                 for r in range(PER_GROUP):
                     nc.tensor.matmul(
-                        flipped_sum[:],
-                        quads[:, :, r],
-                        identity[:],
-                        is_transpose=True,
-                        start=(r == 0),
-                        stop=(r == PER_GROUP - 1),
+                        sum_in_psum[:], identity[:], apart[:, r, :], start=(r == 0), stop=(r == PER_GROUP - 1)
                     )
-                flipped_neurons = work.tile([BLOCKS * NEURONS, P], F32, name="flipped_neurons")
-                nc.scalar.activation(flipped_neurons[:], flipped_sum[:], TANH)
-                neurons_in_psum = groups.tile([P, BLOCKS * NEURONS], F32, name="neurons_in_psum")
-                nc.tensor.transpose(neurons_in_psum[:], flipped_neurons[:], identity[:])
-                nc.scalar.copy(neurons[:].rearrange("p b n -> p (b n)"), neurons_in_psum[:])
+                nc.scalar.activation(neurons[:].rearrange("p b n -> p (b n)"), sum_in_psum[:], TANH)
             nc.sync.dma_start(out_blocks[:, :, k * NEURONS : (k + 1) * NEURONS], neurons[:])
 
         for u in range(UNITS + BEHIND):

@@ -59,7 +59,6 @@ def tile_memorygraph_kernel(tc, x, br_w, w_logit, grp_w, offs, out):
         group_w = [
             held.tile([P, BLOCKS, pieces * BRANCHES], F32, name=f"group_w{g}") for g, pieces in enumerate(LOAD_PIECES)
         ]
-        nc.sync.dma_start(logit_rows[:], w_logit.rearrange("o (m j) -> (o m) j", j=SLAB))
         nc.sync.dma_start(offsets[:], offs)
         for g, (first, pieces) in enumerate(zip(LOAD_FROM, LOAD_PIECES)):
             for b in range(BLOCKS):
@@ -68,6 +67,8 @@ def tile_memorygraph_kernel(tc, x, br_w, w_logit, grp_w, offs, out):
                 nc.sync.dma_start(
                     branch_w[g][b][:], br_w[b * P : (b + 1) * P, first * PIECE : (first + pieces) * PIECE]
                 )
+                if g == 0 and b == 0:
+                    nc.sync.dma_start(logit_rows[:], w_logit.rearrange("o (m j) -> (o m) j", j=SLAB))
             nc.sync.dma_start(group_w[g][:], grp_w_blocks[:, :, first * BRANCHES : (first + pieces) * BRANCHES])
 
         identity = held.tile([P, P], F32, name="identity")

@@ -19,7 +19,6 @@ PER_GROUP = 4
 BLOCKS = C // P
 PIECE = S
 PIECES = N // PIECE
-UNITS = PIECES * BLOCKS
 BRANCHES = PIECE // PER_BRANCH
 NEURONS = BRANCHES // PER_GROUP
 SLAB = P * PER_BRANCH
@@ -28,6 +27,11 @@ SLABS_IN_PIECE = PIECE // SLAB
 LOAD_FROM = [0, 1, 2, 4]
 LOAD_PIECES = [1, 1, 2, 4]
 assert all(LOAD_FROM[g] == sum(LOAD_PIECES[:g]) for g in range(len(LOAD_FROM))) and sum(LOAD_PIECES) == PIECES
+WHOLE = (0, SLABS_IN_PIECE)
+UNITS = [(k, b, WHOLE) for k in range(PIECES) for b in range(BLOCKS)][:-1] + [
+    (PIECES - 1, BLOCKS - 1, (h, h + 1)) for h in range(SLABS_IN_PIECE)
+]
+ON_TENSOR = PIECES - 2
 BEHIND = 3
 
 
@@ -83,21 +87,23 @@ def tile_memorygraph_kernel(tc, x, br_w, w_logit, grp_w, offs, out):
         gate = held.tile([P, PER_BRANCH, SLABS], F32, name="gate")
         nc.scalar.activation(gate[:], logit_columns[:], SIGMOID)
 
-        product, gated, branch = {}, {}, {}
+        product, gated, branch, apart = {}, {}, {}, {}
 
         def look_up(u):
-            k, b = divmod(u, BLOCKS)
-            picked = windows[b][:].indirect(offsets[:, k * (PIECE // 16) : (k + 1) * (PIECE // 16)])
-            product[u] = products.tile([P, PIECE], F32, name="product")
+            k, b, (start, end) = UNITS[u]
+            first, entries = k * PIECE + start * SLAB, (end - start) * SLAB
+            picked = windows[b][:].indirect(offsets[:, first // 16 : (first + entries) // 16])
+            product[u] = products.tile([P, entries], F32, name="product")
             g, i = load_of(k)
-            nc.vector.tensor_tensor(product[u][:], picked, branch_w[g][b][:, i * PIECE : (i + 1) * PIECE], MULT)
+            weights = branch_w[g][b][:, i * PIECE + start * SLAB : i * PIECE + end * SLAB]
+            nc.vector.tensor_tensor(product[u][:], picked, weights, MULT)
 
         def flip_and_gate(u):
-            k = u // BLOCKS
-            by_connection = product[u][:].rearrange("p (h q i) -> p h q i", h=SLABS_IN_PIECE, i=PER_BRANCH)
-            gated[u] = work.tile([P, SLABS_IN_PIECE, PER_BRANCH, P], F32, name="gated")
-            for h in range(SLABS_IN_PIECE):
-                m = k * SLABS_IN_PIECE + h
+            k, b, (start, end) = UNITS[u]
+            by_connection = product[u][:].rearrange("p (h q i) -> p h q i", h=end - start, i=PER_BRANCH)
+            gated[u] = work.tile([P, end - start, PER_BRANCH, P], F32, name="gated")
+            for h in range(end - start):
+                m = k * SLABS_IN_PIECE + start + h
                 flipped = flips.tile([P, PER_BRANCH, P], F32, name="flipped")
                 for i in range(PER_BRANCH):
                     nc.tensor.transpose(flipped[:, i, :], by_connection[:, h, :, i], identity[:])
@@ -105,11 +111,11 @@ def tile_memorygraph_kernel(tc, x, br_w, w_logit, grp_w, offs, out):
                     nc.scalar.activation(gated[u][:, h, i, :], flipped[:, i, :], COPY, scale=gate[:, i, m : m + 1])
 
         def make_branches(u):
-            k, b = divmod(u, BLOCKS)
-            if b == 0:
+            k, b, (start, end) = UNITS[u]
+            if k not in branch:
                 branch[k] = work.tile([P, BLOCKS, BRANCHES], F32, name="branch")
-            branch_sum = sums.tile([P, BRANCHES], F32, name="branch_sum")
-            for h in range(SLABS_IN_PIECE):
+            branch_sum = sums.tile([P, (end - start) * P], F32, name="branch_sum")
+            for h in range(end - start):
                 for i in range(PER_BRANCH):
                     nc.tensor.matmul(
                         branch_sum[:, h * P : (h + 1) * P],
@@ -119,41 +125,57 @@ def tile_memorygraph_kernel(tc, x, br_w, w_logit, grp_w, offs, out):
                         start=(i == 0),
                         stop=(i == PER_BRANCH - 1),
                     )
-            nc.scalar.activation(branch[k][:, b, :], branch_sum[:], TANH)
+            nc.scalar.activation(branch[k][:, b, start * P : end * P], branch_sum[:], TANH)
 
-        def make_neurons(k):
+        def group_weights(k):
             g, i = load_of(k)
-            weights = group_w[g][:, :, i * BRANCHES : (i + 1) * BRANCHES]
-            neurons = held.tile([P, BLOCKS, NEURONS], F32, name=f"neurons{k}")
-            if k == PIECES - 1:
-                grouped = work.tile([P, BLOCKS, BRANCHES], F32, name="grouped")
-                group_sum = work.tile([P, BLOCKS, NEURONS], F32, name="group_sum")
-                for b in range(BLOCKS):
-                    nc.vector.tensor_tensor(grouped[:, b, :], branch[k][:, b, :], weights[:, b, :], MULT)
-                    quads = grouped[:, b, :].rearrange("p (n r) -> p n r", r=PER_GROUP)
-                    nc.vector.tensor_reduce(group_sum[:, b, :], quads, ALONG_ROW, ADD)
-                    nc.scalar.activation(neurons[:, b, :], group_sum[:, b, :], TANH)
-            else:
-                apart = work.tile([P, PER_GROUP, BLOCKS * NEURONS], F32, name="apart")
-                nc.vector.tensor_tensor(
-                    apart[:].rearrange("p r (b n) -> p b n r", b=BLOCKS),
-                    branch[k][:].rearrange("p b (n r) -> p b n r", r=PER_GROUP),
-                    weights.rearrange("p b (n r) -> p b n r", r=PER_GROUP),
-                    MULT,
-                )
-                sum_in_psum = groups.tile([P, BLOCKS * NEURONS], F32, name="sum_in_psum")
-                for r in range(PER_GROUP):
-                    nc.tensor.matmul(
-                        sum_in_psum[:], identity[:], apart[:, r, :], start=(r == 0), stop=(r == PER_GROUP - 1)
-                    )
-                nc.scalar.activation(neurons[:].rearrange("p b n -> p (b n)"), sum_in_psum[:], TANH)
+            return group_w[g][:, :, i * BRANCHES : (i + 1) * BRANCHES]
+
+        def store(k, neurons):
             nc.sync.dma_start(out_blocks[:, :, k * NEURONS : (k + 1) * NEURONS], neurons[:])
 
-        for u in range(UNITS + BEHIND):
-            if u < UNITS:
+        def multiply_branches(k):
+            apart[k] = work.tile([P, PER_GROUP, BLOCKS * NEURONS], F32, name="apart")
+            nc.vector.tensor_tensor(
+                apart[k][:].rearrange("p r (b n) -> p b n r", b=BLOCKS),
+                branch[k][:].rearrange("p b (n r) -> p b n r", r=PER_GROUP),
+                group_weights(k).rearrange("p b (n r) -> p b n r", r=PER_GROUP),
+                MULT,
+            )
+
+        def add_up(k):
+            sum_in_psum = groups.tile([P, BLOCKS * NEURONS], F32, name="sum_in_psum")
+            for r in range(PER_GROUP):
+                nc.tensor.matmul(sum_in_psum[:], identity[:], apart[k][:, r, :], start=(r == 0), stop=(r == PER_GROUP - 1))
+            neurons = held.tile([P, BLOCKS, NEURONS], F32, name=f"neurons{k}")
+            nc.scalar.activation(neurons[:].rearrange("p b n -> p (b n)"), sum_in_psum[:], TANH)
+            store(k, neurons)
+
+        def make_neurons_on_vector(k):
+            grouped = work.tile([P, BLOCKS, BRANCHES], F32, name="grouped")
+            group_sum = work.tile([P, BLOCKS, NEURONS], F32, name="group_sum")
+            for unit_k, b, (start, end) in UNITS:
+                if unit_k == k:
+                    q = slice(start * P, end * P)
+                    n = slice(start * P // PER_GROUP, end * P // PER_GROUP)
+                    nc.vector.tensor_tensor(grouped[:, b, q], branch[k][:, b, q], group_weights(k)[:, b, q], MULT)
+                    quads = grouped[:, b, q].rearrange("p (n r) -> p n r", r=PER_GROUP)
+                    nc.vector.tensor_reduce(group_sum[:, b, n], quads, ALONG_ROW, ADD)
+            neurons = held.tile([P, BLOCKS, NEURONS], F32, name=f"neurons{k}")
+            nc.scalar.activation(neurons[:], group_sum[:], TANH)
+            store(k, neurons)
+
+        for u in range(len(UNITS) + 1):
+            if u < len(UNITS):
                 look_up(u)
                 flip_and_gate(u)
-            if 1 <= u <= UNITS:
+            if u >= 1:
                 make_branches(u - 1)
-            if u > BEHIND and (u - BEHIND) % BLOCKS == 1:
-                make_neurons((u - BEHIND) // BLOCKS)
+            k, b = divmod(u - BEHIND - 1, BLOCKS)
+            if b == 0 and 0 <= k < ON_TENSOR:
+                multiply_branches(k)
+                if k < ON_TENSOR - 1:
+                    add_up(k)
+        add_up(ON_TENSOR - 1)
+        for k in range(ON_TENSOR, PIECES):
+            make_neurons_on_vector(k)

import concourse.mybir as mybir
from concourse.masks import make_identity

F32 = mybir.dt.float32
U16 = mybir.dt.uint16
MULT = mybir.AluOpType.mult
ADD = mybir.AluOpType.add
ALONG_ROW = mybir.AxisListType.X
SIGMOID = mybir.ActivationFunctionType.Sigmoid
TANH = mybir.ActivationFunctionType.Tanh
COPY = mybir.ActivationFunctionType.Copy

P = 128
C = 256
S = 512
N = 4096
PER_BRANCH = 2
PER_GROUP = 4
BLOCKS = C // P
PIECE = S
PIECES = N // PIECE
BRANCHES = PIECE // PER_BRANCH
NEURONS = BRANCHES // PER_GROUP
SLAB = P * PER_BRANCH
SLABS = N // SLAB
SLABS_IN_PIECE = PIECE // SLAB
LOAD_FROM = [0, 1, 2, 4]
LOAD_PIECES = [1, 1, 2, 4]
assert all(LOAD_FROM[g] == sum(LOAD_PIECES[:g]) for g in range(len(LOAD_FROM))) and sum(LOAD_PIECES) == PIECES
WHOLE = (0, SLABS_IN_PIECE)
UNITS = [(k, b, WHOLE) for k in range(PIECES) for b in range(BLOCKS)][:-1] + [
    (PIECES - 1, BLOCKS - 1, (h, h + 1)) for h in range(SLABS_IN_PIECE)
]
ON_TENSOR = PIECES - 2
BEHIND = 3


def load_of(k):
    g = max(g for g in range(len(LOAD_FROM)) if LOAD_FROM[g] <= k)
    return g, k - LOAD_FROM[g]


def tile_memorygraph_kernel(tc, x, br_w, w_logit, grp_w, offs, out):
    nc = tc.nc
    with (
        tc.tile_pool(name="held", bufs=1) as held,
        tc.tile_pool(name="work", bufs=3) as work,
        tc.tile_pool(name="products", bufs=2) as products,
        tc.psum_pool(name="flips", bufs=2 * SLABS_IN_PIECE) as flips,
        tc.psum_pool(name="sums", bufs=2) as sums,
        tc.psum_pool(name="groups", bufs=2) as groups,
    ):
        grp_w_blocks = grp_w.rearrange("(b p) q -> p b q", p=P)
        out_blocks = out.rearrange("(b p) n -> p b n", p=P)

        logit_rows = held.tile([SLABS, SLAB], F32, name="logit_rows")
        offsets = held.tile([P, N // 16], U16, name="offsets")
        windows = [held.tile([P, S], F32, name=f"window{b}") for b in range(BLOCKS)]
        branch_w = [
            [held.tile([P, pieces * PIECE], F32, name=f"branch_w{g}_{b}") for b in range(BLOCKS)]
            for g, pieces in enumerate(LOAD_PIECES)
        ]
        group_w = [
            held.tile([P, BLOCKS, pieces * BRANCHES], F32, name=f"group_w{g}") for g, pieces in enumerate(LOAD_PIECES)
        ]
        nc.sync.dma_start(offsets[:], offs)
        for g, (first, pieces) in enumerate(zip(LOAD_FROM, LOAD_PIECES)):
            for b in range(BLOCKS):
                if g == 0:
                    nc.sync.dma_start(windows[b][:], x[b * P : (b + 1) * P, :])
                nc.sync.dma_start(
                    branch_w[g][b][:], br_w[b * P : (b + 1) * P, first * PIECE : (first + pieces) * PIECE]
                )
                if g == 0 and b == 0:
                    nc.sync.dma_start(logit_rows[:], w_logit.rearrange("o (m j) -> (o m) j", j=SLAB))
            nc.sync.dma_start(group_w[g][:], grp_w_blocks[:, :, first * BRANCHES : (first + pieces) * BRANCHES])

        identity = held.tile([P, P], F32, name="identity")
        make_identity(nc, identity[:])

        logit_columns = groups.tile([P, PER_BRANCH, SLABS], F32, name="logit_columns", tag="sum_in_psum")
        connections = logit_rows[:].rearrange("m (q i) -> m q i", i=PER_BRANCH)
        for i in range(PER_BRANCH):
            nc.tensor.matmul(
                logit_columns[:, i, :], connections[:, :, i], identity[0:SLABS, 0:SLABS], start=True, stop=True
            )
        gate = held.tile([P, PER_BRANCH, SLABS], F32, name="gate")
        nc.scalar.activation(gate[:], logit_columns[:], SIGMOID)

        product, gated, branch, apart = {}, {}, {}, {}

        def look_up(u):
            k, b, (start, end) = UNITS[u]
            first, entries = k * PIECE + start * SLAB, (end - start) * SLAB
            picked = windows[b][:].indirect(offsets[:, first // 16 : (first + entries) // 16])
            product[u] = products.tile([P, entries], F32, name="product")
            g, i = load_of(k)
            weights = branch_w[g][b][:, i * PIECE + start * SLAB : i * PIECE + end * SLAB]
            nc.vector.tensor_tensor(product[u][:], picked, weights, MULT)

        def flip_and_gate(u):
            k, b, (start, end) = UNITS[u]
            by_connection = product[u][:].rearrange("p (h q i) -> p h q i", h=end - start, i=PER_BRANCH)
            gated[u] = work.tile([P, end - start, PER_BRANCH, P], F32, name="gated")
            for h in range(end - start):
                m = k * SLABS_IN_PIECE + start + h
                flipped = flips.tile([P, PER_BRANCH, P], F32, name="flipped")
                for i in range(PER_BRANCH):
                    nc.tensor.transpose(flipped[:, i, :], by_connection[:, h, :, i], identity[:])
                for i in range(PER_BRANCH):
                    nc.scalar.activation(gated[u][:, h, i, :], flipped[:, i, :], COPY, scale=gate[:, i, m : m + 1])

        def make_branches(u):
            k, b, (start, end) = UNITS[u]
            if k not in branch:
                branch[k] = work.tile([P, BLOCKS, BRANCHES], F32, name="branch")
            branch_sum = sums.tile([P, (end - start) * P], F32, name="branch_sum")
            for h in range(end - start):
                for i in range(PER_BRANCH):
                    nc.tensor.matmul(
                        branch_sum[:, h * P : (h + 1) * P],
                        gated[u][:, h, i, :],
                        identity[:],
                        is_transpose=True,
                        start=(i == 0),
                        stop=(i == PER_BRANCH - 1),
                    )
            nc.scalar.activation(branch[k][:, b, start * P : end * P], branch_sum[:], TANH)

        def group_weights(k):
            g, i = load_of(k)
            return group_w[g][:, :, i * BRANCHES : (i + 1) * BRANCHES]

        def store(k, neurons):
            nc.sync.dma_start(out_blocks[:, :, k * NEURONS : (k + 1) * NEURONS], neurons[:])

        def multiply_branches(k):
            apart[k] = work.tile([P, PER_GROUP, BLOCKS * NEURONS], F32, name="apart")
            nc.vector.tensor_tensor(
                apart[k][:].rearrange("p r (b n) -> p b n r", b=BLOCKS),
                branch[k][:].rearrange("p b (n r) -> p b n r", r=PER_GROUP),
                group_weights(k).rearrange("p b (n r) -> p b n r", r=PER_GROUP),
                MULT,
            )

        def add_up(k):
            sum_in_psum = groups.tile([P, BLOCKS * NEURONS], F32, name="sum_in_psum")
            for r in range(PER_GROUP):
                nc.tensor.matmul(sum_in_psum[:], identity[:], apart[k][:, r, :], start=(r == 0), stop=(r == PER_GROUP - 1))
            neurons = held.tile([P, BLOCKS, NEURONS], F32, name=f"neurons{k}")
            nc.scalar.activation(neurons[:].rearrange("p b n -> p (b n)"), sum_in_psum[:], TANH)
            store(k, neurons)

        def make_neurons_on_vector(k):
            grouped = work.tile([P, BLOCKS, BRANCHES], F32, name="grouped")
            group_sum = work.tile([P, BLOCKS, NEURONS], F32, name="group_sum")
            for unit_k, b, (start, end) in UNITS:
                if unit_k == k:
                    q = slice(start * P, end * P)
                    n = slice(start * P // PER_GROUP, end * P // PER_GROUP)
                    nc.vector.tensor_tensor(grouped[:, b, q], branch[k][:, b, q], group_weights(k)[:, b, q], MULT)
                    quads = grouped[:, b, q].rearrange("p (n r) -> p n r", r=PER_GROUP)
                    nc.vector.tensor_reduce(group_sum[:, b, n], quads, ALONG_ROW, ADD)
            neurons = held.tile([P, BLOCKS, NEURONS], F32, name=f"neurons{k}")
            nc.scalar.activation(neurons[:], group_sum[:], TANH)
            store(k, neurons)

        for u in range(len(UNITS) + 1):
            if u < len(UNITS):
                look_up(u)
                flip_and_gate(u)
            if u >= 1:
                make_branches(u - 1)
            k, b = divmod(u - BEHIND - 1, BLOCKS)
            if b == 0 and 0 <= k < ON_TENSOR:
                multiply_branches(k)
                if k < ON_TENSOR - 1:
                    add_up(k)
        add_up(ON_TENSOR - 1)
        for k in range(ON_TENSOR, PIECES):
            make_neurons_on_vector(k)
